import numpy as np
import ml_dtypes


def mxq(x, axis, fmt="e4m3"):
    dtype, down = {"e4m3": (ml_dtypes.float8_e4m3fn, 7), "e5m2": (ml_dtypes.float8_e5m2, 14)}[fmt]
    v = np.moveaxis(np.asarray(x, np.float32).astype(ml_dtypes.bfloat16).astype(np.float64), axis, -1)
    blocks = v.reshape(v.shape[:-1] + (-1, 32))
    amax = np.abs(blocks).max(-1, keepdims=True)
    byte = np.maximum(np.where(amax > 0, np.frexp(amax)[1] - 1 + 127, 0) - down, 1)
    scale = np.exp2(byte - 127.0)
    codes = (blocks / scale).astype(np.float32).astype(dtype).astype(np.float64)
    return np.moveaxis((codes * scale).reshape(v.shape), -1, axis)


WIDE = False


def mx_kscale(k):
    if not WIDE:
        return np.ones(k)
    levels = np.array([10, -10, 5, -5, 0])
    a = np.random.permutation(np.resize(levels, k // 512 * 4)).reshape(k // 512, 4)
    idx = np.arange(k)
    return np.exp2(a[idx // 512, idx % 128 // 32])


BF16 = ml_dtypes.bfloat16


def bf(x):
    return np.asarray(x, np.float32).astype(BF16)


def f64(x):
    return np.asarray(x).astype(np.float64)


B, N, D, P, Z = 1, 128, 1024, 511, 32
P1 = P + 1


def leaky_draw(shape):
    g = np.random.standard_normal(shape)
    return np.where(g > 0.0, g, 0.1 * g)


def with_ones(v):
    return np.concatenate([v, np.ones(v.shape[:-1] + (1,))], axis=-1)


def setup_inputs():
    s, u = mx_kscale(P1), mx_kscale(P1)
    s, u = s / s[-1], u / u[-1]
    return {"xp": bf(leaky_draw((B, N, P)) * s[:P]),
            "yp": bf(leaky_draw((B, N, P)) / u[:P]),
            "w": bf(np.random.standard_normal((B, Z, P1, P1)) * 0.36 / np.sqrt(P1) / s[:, None] * u)}


def reference(xp, yp, w):
    x1 = mxq(with_ones(f64(xp)), 2, "e4m3")
    y1 = mxq(with_ones(f64(yp)), 2, "e4m3")
    t = x1[:, None] @ mxq(f64(w), 2, "e4m3")
    sc = mxq(t, 3, "e4m3") @ y1.transpose(0, 2, 1)[:, None]
    return sc.transpose(0, 2, 3, 1)

@@ -1,0 +1,178 @@
+from contextlib import ExitStack
+
+import concourse.masks as masks
+import concourse.mybir as mybir
+
+BF16 = mybir.dt.bfloat16
+F32 = mybir.dt.float32
+U32 = mybir.dt.uint32
+U8 = mybir.dt.uint8
+FP8X4 = mybir.dt.float8_e4m3fn_x4
+
+P = 128
+PACK = 4
+K = P * PACK
+N_MAPS = 32
+GROUP = 4
+N_GROUPS = N_MAPS // GROUP
+
+FLOPS = 2 * N_MAPS * P * K * K + 2 * N_MAPS * P * P * K
+
+RUN = 4
+N_RUNS = K // RUN
+VECTOR_RUNS = 84
+
+ROUND_LAG = 2
+SECOND_LAG = 3
+GATHER_LAG = 5
+
+STORE_CHUNKS = 4
+
+
+def load_with_ones(nc, pool, feats, name):
+    full = pool.tile([P, K], BF16, name=name)
+    nc.vector.memset(full[:, K - 16 : K], 1.0)
+    nc.scalar.dma_start(out=full[:, 0 : K - 1], in_=feats.rearrange("b n f -> (b n) f"))
+    return full
+
+
+def transpose_and_quantise(nc, psum, pool, planes, ident, name):
+    turned = psum.tile([P, PACK, P], BF16, name="turned")
+    for t in range(PACK):
+        nc.tensor.transpose(turned[:, t, :], planes[:, t, :], ident[:])
+    grouped = pool.tile([P, P, PACK], BF16, name=name + "_grouped", align_bytes=64)
+    nc.scalar.copy(out=grouped[:], in_=turned[:].rearrange("p t n -> p n t"))
+    codes = pool.tile([P, P], U32, name=name + "_codes", align_bytes=64)
+    scales = pool.tile([P, P], U8, name=name + "_scales", align_bytes=64)
+    nc.vector.quantize_mx(
+        out=codes[:].bitcast(FP8X4),
+        scales=scales[:],
+        in_=grouped[:].rearrange("p n t -> p (n t)"),
+    )
+    return codes, scales
+
+
+def tile_span2oscorer_pa_kernel(tc, xp, yp, w, out):
+    nc = tc.nc
+    with ExitStack() as ctx:
+        keep = ctx.enter_context(tc.tile_pool(name="keep", bufs=1))
+        raw_pool = ctx.enter_context(tc.tile_pool(name="raw", bufs=N_MAPS))
+        map_pool = ctx.enter_context(tc.tile_pool(name="map", bufs=3))
+        t_pool = ctx.enter_context(tc.tile_pool(name="t", bufs=2))
+        psum_turn = ctx.enter_context(tc.psum_pool(name="psum_turn", bufs=2))
+        psum_t = ctx.enter_context(tc.psum_pool(name="psum_t", bufs=4))
+        psum_out = ctx.enter_context(tc.psum_pool(name="psum_out", bufs=2))
+        ctx.enter_context(tc.manual_schedule())
+
+        x1 = load_with_ones(nc, keep, xp, "x1")
+        y1 = load_with_ones(nc, keep, yp, "y1")
+        raw = []
+        for z in range(N_MAPS):
+            raw_z = raw_pool.tile([P, PACK, K], BF16, name="raw_z")
+            nc.sync.dma_start(out=raw_z[:], in_=w[0, z].rearrange("(p t) j -> p t j", t=PACK))
+            raw.append(raw_z)
+
+        ident = keep.tile([P, P], BF16, name="ident")
+        masks.make_identity(nc, ident[:])
+        out_sb = keep.tile([P, P, N_MAPS], F32, name="out_sb")
+        out_rows = out.rearrange("b x y z -> (b x) y z")
+
+        map_grouped = {}
+        t_bank = {}
+        t_grouped = {}
+        out_bank = {}
+
+        def regroup(z):
+            grouped = map_pool.tile([P, K, PACK], BF16, name="map_grouped", align_bytes=64)
+            src = raw[z][:].rearrange("p t (c i) -> p c t i", i=RUN)
+            dst = grouped[:].rearrange("p (c i) t -> p c t i", i=RUN)
+            nc.vector.tensor_copy(out=dst[:, :VECTOR_RUNS], in_=src[:, :VECTOR_RUNS])
+            nc.scalar.copy(out=dst[:, VECTOR_RUNS:], in_=src[:, VECTOR_RUNS:])
+            map_grouped[z] = grouped
+
+        def first_product(z):
+            codes = map_pool.tile([P, K], U32, name="map_codes", align_bytes=64)
+            scales = map_pool.tile([P, K], U8, name="map_scales", align_bytes=64)
+            nc.vector.quantize_mx(
+                out=codes[:].bitcast(FP8X4),
+                scales=scales[:],
+                in_=map_grouped[z][:].rearrange("p j t -> p (j t)"),
+            )
+            bank = psum_t.tile([P, PACK, P], F32, name="t_bank")
+            for b in range(PACK):
+                j_cols = slice(b * P, (b + 1) * P)
+                nc.tensor.matmul_mx(
+                    out=bank[:, b, :],
+                    lhsT=codes[:, j_cols].bitcast(FP8X4),
+                    lhsT_scale=scales[:, j_cols],
+                    rhs=x_codes[:].bitcast(FP8X4),
+                    rhs_scale=x_scales[:],
+                    start=True,
+                    stop=True,
+                )
+            t_bank[z] = bank
+
+        def round_t(z):
+            g = z // GROUP
+            if z % GROUP == 0:
+                t_grouped[g] = t_pool.tile([P, GROUP, P, PACK], BF16, name="t_grouped", align_bytes=64)
+            nc.scalar.copy(out=t_grouped[g][:, z % GROUP], in_=t_bank[z][:].rearrange("p b x -> p x b"))
+
+        def second_product(g):
+            codes = t_pool.tile([P, GROUP * P], U32, name="t_codes", align_bytes=64)
+            scales = t_pool.tile([P, GROUP * P], U8, name="t_scales", align_bytes=64)
+            nc.vector.quantize_mx(
+                out=codes[:].bitcast(FP8X4),
+                scales=scales[:],
+                in_=t_grouped[g][:].rearrange("p m x b -> p (m x b)"),
+            )
+            bank = psum_out.tile([P, GROUP, P], F32, name="out_bank")
+            for m in range(GROUP):
+                x_cols = slice(m * P, (m + 1) * P)
+                nc.tensor.matmul_mx(
+                    out=bank[:, m, :],
+                    lhsT=codes[:, x_cols].bitcast(FP8X4),
+                    lhsT_scale=scales[:, x_cols],
+                    rhs=y_codes[:].bitcast(FP8X4),
+                    rhs_scale=y_scales[:],
+                    start=True,
+                    stop=True,
+                )
+            out_bank[g] = bank
+
+        def gather(g, ys):
+            nc.scalar.copy(
+                out=out_sb[:, ys, g * GROUP : (g + 1) * GROUP],
+                in_=out_bank[g][:, :, ys].rearrange("p m y -> p y m"),
+            )
+
+        def maps_at(z):
+            return [z] if 0 <= z < N_MAPS else []
+
+        def groups_ending_at(z):
+            return [z // GROUP] if 0 <= z < N_MAPS and z % GROUP == GROUP - 1 else []
+
+        regroup(0)
+        x_codes, x_scales = transpose_and_quantise(
+            nc, psum_turn, keep, x1[:].rearrange("n (p t) -> n t p", t=PACK), ident, "x"
+        )
+        y_codes, y_scales = transpose_and_quantise(
+            nc, psum_turn, keep, y1[:].rearrange("n (b p) -> n b p", b=PACK), ident, "y"
+        )
+        for step in range(N_MAPS + SECOND_LAG):
+            for z in maps_at(step + 1):
+                regroup(z)
+            for z in maps_at(step):
+                first_product(z)
+            for z in maps_at(step - ROUND_LAG):
+                round_t(z)
+            for g in groups_ending_at(step - SECOND_LAG):
+                second_product(g)
+            for g in groups_ending_at(step - GATHER_LAG):
+                gather(g, slice(0, P))
+
+        y_chunk = P // STORE_CHUNKS
+        for c in range(STORE_CHUNKS):
+            ys = slice(c * y_chunk, (c + 1) * y_chunk)
+            gather(N_GROUPS - 1, ys)
+            nc.sync.dma_start(out=out_rows[:, ys, :], in_=out_sb[:, ys, :])

@@ -57,20 +57,19 @@ def tile_span2oscorer_pa_kernel(tc, xp, yp, w, out):
     with ExitStack() as ctx:
         keep = ctx.enter_context(tc.tile_pool(name="keep", bufs=1))
         raw_pool = ctx.enter_context(tc.tile_pool(name="raw", bufs=N_MAPS))
-        map_pool = ctx.enter_context(tc.tile_pool(name="map", bufs=3))
-        t_pool = ctx.enter_context(tc.tile_pool(name="t", bufs=2))
+        map_pool = ctx.enter_context(tc.tile_pool(name="map", bufs=4))
+        t_pool = ctx.enter_context(tc.tile_pool(name="t", bufs=3))
         psum_turn = ctx.enter_context(tc.psum_pool(name="psum_turn", bufs=2))
         psum_t = ctx.enter_context(tc.psum_pool(name="psum_t", bufs=4))
         psum_out = ctx.enter_context(tc.psum_pool(name="psum_out", bufs=2))
-        ctx.enter_context(tc.manual_schedule())
 
-        x1 = load_with_ones(nc, keep, xp, "x1")
-        y1 = load_with_ones(nc, keep, yp, "y1")
         raw = []
         for z in range(N_MAPS):
             raw_z = raw_pool.tile([P, PACK, K], BF16, name="raw_z")
             nc.sync.dma_start(out=raw_z[:], in_=w[0, z].rearrange("(p t) j -> p t j", t=PACK))
             raw.append(raw_z)
+        x1 = load_with_ones(nc, keep, xp, "x1")
+        y1 = load_with_ones(nc, keep, yp, "y1")
 
         ident = keep.tile([P, P], BF16, name="ident")
         masks.make_identity(nc, ident[:])

@@ -20,11 +20,11 @@ FLOPS = 2 * N_MAPS * P * K * K + 2 * N_MAPS * P * P * K
 
 RUN = 4
 N_RUNS = K // RUN
-VECTOR_RUNS = 84
+VECTOR_RUNS = 82
 
 ROUND_LAG = 2
-SECOND_LAG = 3
-GATHER_LAG = 5
+SECOND_LAG = 15
+GATHER_LAG = 17
 
 STORE_CHUNKS = 4
 
@@ -37,7 +37,7 @@ def load_with_ones(nc, pool, feats, name):
 
 
 def transpose_and_quantise(nc, psum, pool, planes, ident, name):
-    turned = psum.tile([P, PACK, P], BF16, name="turned")
+    turned = psum.tile([P, PACK, P], BF16, name="turned", tag="t_bank")
     for t in range(PACK):
         nc.tensor.transpose(turned[:, t, :], planes[:, t, :], ident[:])
     grouped = pool.tile([P, P, PACK], BF16, name=name + "_grouped", align_bytes=64)
@@ -58,10 +58,9 @@ def tile_span2oscorer_pa_kernel(tc, xp, yp, w, out):
         keep = ctx.enter_context(tc.tile_pool(name="keep", bufs=1))
         raw_pool = ctx.enter_context(tc.tile_pool(name="raw", bufs=N_MAPS))
         map_pool = ctx.enter_context(tc.tile_pool(name="map", bufs=4))
-        t_pool = ctx.enter_context(tc.tile_pool(name="t", bufs=3))
-        psum_turn = ctx.enter_context(tc.psum_pool(name="psum_turn", bufs=2))
+        t_pool = ctx.enter_context(tc.tile_pool(name="t", bufs=6))
         psum_t = ctx.enter_context(tc.psum_pool(name="psum_t", bufs=4))
-        psum_out = ctx.enter_context(tc.psum_pool(name="psum_out", bufs=2))
+        psum_out = ctx.enter_context(tc.psum_pool(name="psum_out", bufs=4))
 
         raw = []
         for z in range(N_MAPS):
@@ -153,10 +152,10 @@ def tile_span2oscorer_pa_kernel(tc, xp, yp, w, out):
 
         regroup(0)
         x_codes, x_scales = transpose_and_quantise(
-            nc, psum_turn, keep, x1[:].rearrange("n (p t) -> n t p", t=PACK), ident, "x"
+            nc, psum_t, keep, x1[:].rearrange("n (p t) -> n t p", t=PACK), ident, "x"
         )
         y_codes, y_scales = transpose_and_quantise(
-            nc, psum_turn, keep, y1[:].rearrange("n (b p) -> n b p", b=PACK), ident, "y"
+            nc, psum_t, keep, y1[:].rearrange("n (b p) -> n b p", b=PACK), ident, "y"
         )
         for step in range(N_MAPS + SECOND_LAG):
             for z in maps_at(step + 1):

@@ -61,6 +61,7 @@ def tile_span2oscorer_pa_kernel(tc, xp, yp, w, out):
         t_pool = ctx.enter_context(tc.tile_pool(name="t", bufs=6))
         psum_t = ctx.enter_context(tc.psum_pool(name="psum_t", bufs=4))
         psum_out = ctx.enter_context(tc.psum_pool(name="psum_out", bufs=4))
+        ctx.enter_context(tc.manual_schedule())
 
         raw = []
         for z in range(N_MAPS):

from contextlib import ExitStack

import concourse.masks as masks
import concourse.mybir as mybir

BF16 = mybir.dt.bfloat16
F32 = mybir.dt.float32
U32 = mybir.dt.uint32
U8 = mybir.dt.uint8
FP8X4 = mybir.dt.float8_e4m3fn_x4

P = 128
PACK = 4
K = P * PACK
N_MAPS = 32
GROUP = 4
N_GROUPS = N_MAPS // GROUP

FLOPS = 2 * N_MAPS * P * K * K + 2 * N_MAPS * P * P * K

RUN = 4
N_RUNS = K // RUN
VECTOR_RUNS = 82

ROUND_LAG = 2
SECOND_LAG = 15
GATHER_LAG = 17

STORE_CHUNKS = 4


def load_with_ones(nc, pool, feats, name):
    full = pool.tile([P, K], BF16, name=name)
    nc.vector.memset(full[:, K - 16 : K], 1.0)
    nc.scalar.dma_start(out=full[:, 0 : K - 1], in_=feats.rearrange("b n f -> (b n) f"))
    return full


def transpose_and_quantise(nc, psum, pool, planes, ident, name):
    turned = psum.tile([P, PACK, P], BF16, name="turned", tag="t_bank")
    for t in range(PACK):
        nc.tensor.transpose(turned[:, t, :], planes[:, t, :], ident[:])
    grouped = pool.tile([P, P, PACK], BF16, name=name + "_grouped", align_bytes=64)
    nc.scalar.copy(out=grouped[:], in_=turned[:].rearrange("p t n -> p n t"))
    codes = pool.tile([P, P], U32, name=name + "_codes", align_bytes=64)
    scales = pool.tile([P, P], U8, name=name + "_scales", align_bytes=64)
    nc.vector.quantize_mx(
        out=codes[:].bitcast(FP8X4),
        scales=scales[:],
        in_=grouped[:].rearrange("p n t -> p (n t)"),
    )
    return codes, scales


def tile_span2oscorer_pa_kernel(tc, xp, yp, w, out):
    nc = tc.nc
    with ExitStack() as ctx:
        keep = ctx.enter_context(tc.tile_pool(name="keep", bufs=1))
        raw_pool = ctx.enter_context(tc.tile_pool(name="raw", bufs=N_MAPS))
        map_pool = ctx.enter_context(tc.tile_pool(name="map", bufs=4))
        t_pool = ctx.enter_context(tc.tile_pool(name="t", bufs=6))
        psum_t = ctx.enter_context(tc.psum_pool(name="psum_t", bufs=4))
        psum_out = ctx.enter_context(tc.psum_pool(name="psum_out", bufs=4))
        ctx.enter_context(tc.manual_schedule())

        raw = []
        for z in range(N_MAPS):
            raw_z = raw_pool.tile([P, PACK, K], BF16, name="raw_z")
            nc.sync.dma_start(out=raw_z[:], in_=w[0, z].rearrange("(p t) j -> p t j", t=PACK))
            raw.append(raw_z)
        x1 = load_with_ones(nc, keep, xp, "x1")
        y1 = load_with_ones(nc, keep, yp, "y1")

        ident = keep.tile([P, P], BF16, name="ident")
        masks.make_identity(nc, ident[:])
        out_sb = keep.tile([P, P, N_MAPS], F32, name="out_sb")
        out_rows = out.rearrange("b x y z -> (b x) y z")

        map_grouped = {}
        t_bank = {}
        t_grouped = {}
        out_bank = {}

        def regroup(z):
            grouped = map_pool.tile([P, K, PACK], BF16, name="map_grouped", align_bytes=64)
            src = raw[z][:].rearrange("p t (c i) -> p c t i", i=RUN)
            dst = grouped[:].rearrange("p (c i) t -> p c t i", i=RUN)
            nc.vector.tensor_copy(out=dst[:, :VECTOR_RUNS], in_=src[:, :VECTOR_RUNS])
            nc.scalar.copy(out=dst[:, VECTOR_RUNS:], in_=src[:, VECTOR_RUNS:])
            map_grouped[z] = grouped

        def first_product(z):
            codes = map_pool.tile([P, K], U32, name="map_codes", align_bytes=64)
            scales = map_pool.tile([P, K], U8, name="map_scales", align_bytes=64)
            nc.vector.quantize_mx(
                out=codes[:].bitcast(FP8X4),
                scales=scales[:],
                in_=map_grouped[z][:].rearrange("p j t -> p (j t)"),
            )
            bank = psum_t.tile([P, PACK, P], F32, name="t_bank")
            for b in range(PACK):
                j_cols = slice(b * P, (b + 1) * P)
                nc.tensor.matmul_mx(
                    out=bank[:, b, :],
                    lhsT=codes[:, j_cols].bitcast(FP8X4),
                    lhsT_scale=scales[:, j_cols],
                    rhs=x_codes[:].bitcast(FP8X4),
                    rhs_scale=x_scales[:],
                    start=True,
                    stop=True,
                )
            t_bank[z] = bank

        def round_t(z):
            g = z // GROUP
            if z % GROUP == 0:
                t_grouped[g] = t_pool.tile([P, GROUP, P, PACK], BF16, name="t_grouped", align_bytes=64)
            nc.scalar.copy(out=t_grouped[g][:, z % GROUP], in_=t_bank[z][:].rearrange("p b x -> p x b"))

        def second_product(g):
            codes = t_pool.tile([P, GROUP * P], U32, name="t_codes", align_bytes=64)
            scales = t_pool.tile([P, GROUP * P], U8, name="t_scales", align_bytes=64)
            nc.vector.quantize_mx(
                out=codes[:].bitcast(FP8X4),
                scales=scales[:],
                in_=t_grouped[g][:].rearrange("p m x b -> p (m x b)"),
            )
            bank = psum_out.tile([P, GROUP, P], F32, name="out_bank")
            for m in range(GROUP):
                x_cols = slice(m * P, (m + 1) * P)
                nc.tensor.matmul_mx(
                    out=bank[:, m, :],
                    lhsT=codes[:, x_cols].bitcast(FP8X4),
                    lhsT_scale=scales[:, x_cols],
                    rhs=y_codes[:].bitcast(FP8X4),
                    rhs_scale=y_scales[:],
                    start=True,
                    stop=True,
                )
            out_bank[g] = bank

        def gather(g, ys):
            nc.scalar.copy(
                out=out_sb[:, ys, g * GROUP : (g + 1) * GROUP],
                in_=out_bank[g][:, :, ys].rearrange("p m y -> p y m"),
            )

        def maps_at(z):
            return [z] if 0 <= z < N_MAPS else []

        def groups_ending_at(z):
            return [z // GROUP] if 0 <= z < N_MAPS and z % GROUP == GROUP - 1 else []

        regroup(0)
        x_codes, x_scales = transpose_and_quantise(
            nc, psum_t, keep, x1[:].rearrange("n (p t) -> n t p", t=PACK), ident, "x"
        )
        y_codes, y_scales = transpose_and_quantise(
            nc, psum_t, keep, y1[:].rearrange("n (b p) -> n b p", b=PACK), ident, "y"
        )
        for step in range(N_MAPS + SECOND_LAG):
            for z in maps_at(step + 1):
                regroup(z)
            for z in maps_at(step):
                first_product(z)
            for z in maps_at(step - ROUND_LAG):
                round_t(z)
            for g in groups_ending_at(step - SECOND_LAG):
                second_product(g)
            for g in groups_ending_at(step - GATHER_LAG):
                gather(g, slice(0, P))

        y_chunk = P // STORE_CHUNKS
        for c in range(STORE_CHUNKS):
            ys = slice(c * y_chunk, (c + 1) * y_chunk)
            gather(N_GROUPS - 1, ys)
            nc.sync.dma_start(out=out_rows[:, ys, :], in_=out_sb[:, ys, :])
